import numpy as np
import ml_dtypes


def mxq(x, axis, fmt="e4m3"):
    dtype, down = {"e4m3": (ml_dtypes.float8_e4m3fn, 7), "e5m2": (ml_dtypes.float8_e5m2, 14)}[fmt]
    v = np.moveaxis(np.asarray(x, np.float32).astype(ml_dtypes.bfloat16).astype(np.float64), axis, -1)
    blocks = v.reshape(v.shape[:-1] + (-1, 32))
    amax = np.abs(blocks).max(-1, keepdims=True)
    byte = np.maximum(np.where(amax > 0, np.frexp(amax)[1] - 1 + 127, 0) - down, 1)
    scale = np.exp2(byte - 127.0)
    codes = (blocks / scale).astype(np.float32).astype(dtype).astype(np.float64)
    return np.moveaxis((codes * scale).reshape(v.shape), -1, axis)


WIDE = False


def mx_kscale(k):
    if not WIDE:
        return np.ones(k)
    levels = np.array([10, -10, 5, -5, 0])
    if k % 512:
        return np.exp2(np.random.permutation(np.resize(levels, k // 32))).repeat(32)
    a = np.empty((k // 512, 16))
    for p in range(k // 512):
        a[p, :8] = np.random.permutation(np.resize(levels, 8))
        for g in range(8):
            far = levels[np.abs(levels - a[p, g]) >= 10]
            a[p, g + 8] = far[np.random.randint(len(far))]
    return np.exp2(a.ravel()).repeat(32)


BF16 = ml_dtypes.bfloat16


def bf(x):
    return np.asarray(x, np.float32).astype(BF16)


def f64(x):
    return np.asarray(x).astype(np.float64)


B, IN, H = 512, 1024, 1024


def sigmoid(v):
    return 1.0 / (1.0 + np.exp(-v))


def draw0():
    s, t = mx_kscale(IN), mx_kscale(H)
    wsc = np.sqrt(2.0 / (IN + H))
    usc = 1.0 / np.sqrt(H)
    return {"joint_h": bf(np.random.standard_normal((B, H)) * t),
            "mgn_h": bf(np.random.standard_normal((B, IN)) * s),
            "W_r": bf(np.random.standard_normal((IN, H)) * wsc / s[:, None]),
            "W_h": bf(np.random.standard_normal((IN, H)) * wsc / s[:, None]),
            "U_r": bf(np.random.standard_normal((H, H)) * usc / t[:, None]),
            "U_h": bf(np.random.standard_normal((H, H)) * usc / t[:, None]),
            "b_r": bf(np.random.standard_normal(H) * 0.5),
            "b_h": bf(np.random.standard_normal(H) * 0.5)}


def core(joint_h, mgn_h, W_r, W_h, U_r, U_h, b_r, b_h):
    h = f64(joint_h)
    xq = mxq(f64(mgn_h), 1, "e4m3")
    r = sigmoid((xq @ mxq(f64(W_r), 0, "e4m3")) + (mxq(h, 1, "e4m3") @ mxq(f64(U_r), 0, "e4m3")) + f64(b_r))
    g = h * r
    return np.tanh((xq @ mxq(f64(W_h), 0, "e4m3")) + (mxq(g, 1, "e4m3") @ mxq(f64(U_h), 0, "e4m3")) + f64(b_h))


def e4m3fn_bytes(y):
    return np.clip(np.asarray(y, np.float64), -448.0, 448.0).astype(np.float32).astype(ml_dtypes.float8_e4m3fn).view(np.uint8)


def e4m3fn_values(b):
    return np.asarray(b, np.uint8).view(ml_dtypes.float8_e4m3fn).astype(np.float64)


def setup_inputs():
    d = draw0()
    x0 = np.asarray(d['W_r']).astype(np.float64)
    s = (np.max(np.abs(x0), axis=(1,), keepdims=True) / 448.0).astype(np.float32)
    out = {}
    for k, v in d.items():
        if k == 'W_r':
            out['W_r_bytes'] = e4m3fn_bytes(x0 / s.astype(np.float64))
            out['W_r_scale'] = s
        else:
            out[k] = v
    return out


def reference(joint_h, mgn_h, W_r_bytes, W_r_scale, W_h, U_r, U_h, b_r, b_h):
    return core(joint_h, mgn_h, e4m3fn_values(W_r_bytes) * W_r_scale.astype(np.float64), W_h, U_r, U_h, b_r, b_h)

@@ -1,0 +1,210 @@
+from contextlib import ExitStack
+
+import concourse.mybir as mybir
+from concourse.masks import make_identity
+
+F32 = mybir.dt.float32
+BF16 = mybir.dt.bfloat16
+U32 = mybir.dt.uint32
+U8 = mybir.dt.uint8
+FP8 = mybir.dt.float8_e4m3fn
+FP8X4 = mybir.dt.float8_e4m3fn_x4
+ACT = mybir.ActivationFunctionType
+ALU = mybir.AluOpType
+
+B, K, H = 512, 1024, 1024
+FLOPS = 4 * 2 * B * K * H
+P = 128
+PASS = 512
+
+LOADS = "R0 R1 U1a x3 h2 x1 U1b h3 h1 U0a x0 x2 h0 H0 U0b H1 V0 V1"
+ORDER = (
+    "WR0b/v WR0a/s WR1b/v WR1a/s IR0b/v IR1b/v IU1a/s IR0a/v Th3 QR1b Tx3 Tx1 QR0a IR1a/s Th1 QU1a "
+    "IU1b/v Tx2 Th2 Cx2/s Ch1/v Tx0 Cx1/s Cx3/v Th0 Ch2/s QR1a Ch0/s IU0a/v Cx0/s Ch3/s Qx0 IU0b/s "
+    "Qx1 mR0a Qh1 QR0b mR1a Qh0 IH00/s QU0b mU1a QU0a mU0b IH10/v mU0a IH11/s IV00/v mR1b sa3 QH10 "
+    "sa2 QU1b mR0b sa0 QV00 sa1 QH11 mU1b IH01/s ga0 sb3 IV01/v sb1 ga1 sb0 IV12/s IH12/v QH00 sb2 "
+    "QV01 Qga IV10/s nH11_2 nH00_1 gb1 nH00_0 nV00_1 nV01_3 nH10_0 nH00_2 gb0 nV00_2 nH10_1 nV01_1 "
+    "IV11/s nV00_3 Qgb nV00_0 nH10_3 QV10 nV01_0 nH10_2 IV02/s nH00_3 QH01 nH11_1 nV10_3 QV11 nV10_1 "
+    "QV12 nH01_2 b03 nV11_1 IH02/s nH01_3 nV11_2 nV10_2 QH12 nH11_0 nV10_0 b02 t03 b00 nV12_2 nH12_3 "
+    "nV11_0 t02 nV01_2 QV02 b01 nV02_2 t00 nV12_3 nH01_0 nV02_0 b12 nV02_3 t01 nH11_3 QH02 nH01_1 "
+    "nH12_2 b11 nV12_0 t12 nV12_1 b10 nV11_3 t11 nH02_0 b13 nH02_2 t10 nH12_0 b22 nH12_1 t13 nV02_1 "
+    "b20 nH02_3 t22 nH02_1 b23 t20 b21 t23 t21 "
+)
+BLOCKS = {"a": (0, 512), "b": (512, 512), "0": (0, 512), "1": (512, 256), "2": (768, 256)}
+
+
+def tile_joint_gru_pa_kernel(tc, joint_h, mgn_h, W_r_bytes, W_r_scale, W_h, U_r, U_h, b_r, b_h, out):
+    nc = tc.nc
+    with ExitStack() as ctx:
+        keep = ctx.enter_context(tc.tile_pool(name="keep", bufs=1))
+        ring = ctx.enter_context(tc.tile_pool(name="ring", bufs=8))
+        psum = ctx.enter_context(tc.psum_pool(name="psum", bufs=1))
+
+        ident = keep.tile([P, P], F32, name="ident")
+        make_identity(nc, ident[:])
+        warm = keep.tile([P, 1], F32, name="warm")
+        nc.vector.memset(warm[:], 0.0)
+
+        ctx.enter_context(tc.manual_schedule())
+        nc.scalar.activation(out=warm[:], in_=warm[:], func=ACT.Sigmoid)
+        w_scale = keep.tile([P, 2, 4], F32, name="w_scale")
+        nc.scalar.dma_start(out=w_scale[:], in_=W_r_scale.rearrange("(g p j) o -> p g (j o)", g=2, j=4))
+        br = keep.tile([P, 2, 4], BF16, name="br")
+        nc.scalar.dma_start(out=br[:], in_=b_r.rearrange("(g p t) -> p g t", g=2, t=4))
+
+        raw = {}
+        for key in LOADS.split():
+            kind, g = key[0], int(key[1])
+            rows = slice(g * PASS, (g + 1) * PASS)
+            if kind in "hx":
+                source = joint_h if kind == "h" else mgn_h
+                t = keep.tile([P, K], BF16, name="raw_" + key)
+                nc.sync.dma_start(out=t[:], in_=source[g * P : (g + 1) * P, :])
+                raw[key] = t
+            elif kind == "R":
+                t = keep.tile([P, 4, H], U8, name="raw_" + key)
+                view = W_r_bytes[rows, :].rearrange("(p j) c -> p j c", j=4)
+                if g == 0:
+                    for j in range(4):
+                        nc.sync.dma_start(out=t[:, j, :], in_=view[:, j, :])
+                else:
+                    nc.sync.dma_start(out=t[:], in_=view)
+                raw[key] = t
+            elif kind == "U":
+                c0, width = BLOCKS[key[2]]
+                t = keep.tile([P, 4, width], BF16, name="raw_" + key)
+                nc.sync.dma_start(out=t[:], in_=U_r[rows, c0 : c0 + width].rearrange("(p j) c -> p j c", j=4))
+                raw[key] = t
+            else:
+                source = W_h if kind == "H" else U_h
+                t = keep.tile([P, 4, H], BF16, name="raw_" + key)
+                nc.sync.dma_start(out=t[:], in_=source[rows, :].rearrange("(p j) c -> p j c", j=4))
+                raw[key] = t
+        bh = keep.tile([P, H], BF16, name="bh")
+        nc.sync.dma_start(out=bh[:], in_=b_h.partition_broadcast(P))
+
+        turned = {}
+        for k in "hx":
+            turned[k] = keep.tile([P, 2 * B * 4], BF16, name="turned_" + k, align_bytes=64)
+        gate = {}
+        for k in "ab":
+            gate[k] = keep.tile([P, 4, B], F32, name="gate_" + k)
+        gated = {}
+        for k in "ab":
+            gated[k] = keep.tile([P, B * 4], BF16, name="gated_" + k, align_bytes=64)
+        wide = {}
+        grouped = {}
+        codes = {}
+        turning = {}
+        acc = {}
+        passes = {}
+        res = {}
+
+        def quant(key, src, width):
+            c = keep.tile([P, width], U32, name="codes_" + key, align_bytes=64)
+            s = keep.tile([P, width], U8, name="scales_" + key, align_bytes=64)
+            nc.vector.quantize_mx(out=c[:].bitcast(FP8X4), scales=s[:], in_=src)
+            codes[key] = (c, s)
+
+        def mx(key, bank, width, left, lcols, right, n, total):
+            if key not in passes:
+                passes[key] = 0
+                acc[key] = psum.tile([P, width], F32, name="acc_" + key, tag=bank)
+            done = passes[key]
+            passes[key] = done + 1
+            nc.tensor.matmul_mx(
+                out=acc[key][:],
+                lhsT=codes[left][0][:, lcols].bitcast(FP8X4),
+                lhsT_scale=codes[left][1][:, lcols],
+                rhs=codes[right][0][:, 0:n].bitcast(FP8X4),
+                rhs_scale=codes[right][1][:, 0:n],
+                start=(done == 0),
+                stop=(done == total - 1),
+            )
+
+        for token in ORDER.split():
+            op = token[0]
+            engine = token[-1] if "/" in token else ""
+            key = token[1:].split("/")[0]
+            if op == "T":
+                t = psum.tile([P, 2, 2, P], F32, name="turning_" + key, tag=("hi" if key[0] == "h" else "lo") + key[1])
+                words = raw[key][:].bitcast(F32)
+                for g in range(2):
+                    for u in range(2):
+                        nc.tensor.transpose(t[:, g, u, :], words[:, 256 * g + u : 256 * (g + 1) : 2], ident[:])
+                turning[key] = t
+            elif op == "C":
+                i = int(key[1])
+                dst = turned[key[0]][:].bitcast(F32).rearrange("p (g r u) -> p g r u", g=2, u=2)[:, :, i * P : (i + 1) * P, :]
+                src = turning[key][:].rearrange("p g u r -> p g r u")
+                if engine == "v":
+                    nc.vector.tensor_copy(out=dst, in_=src)
+                else:
+                    nc.scalar.copy(out=dst, in_=src)
+            elif op == "W":
+                g = int(key[1])
+                c0, width = BLOCKS[key[2]]
+                w = ring.tile([P, 4, 512], BF16, name="wide", tag="wide", bufs=4)
+                for j in range(4):
+                    src = raw["R" + key[1]][:, j, c0 : c0 + width].bitcast(FP8)
+                    if engine == "v":
+                        nc.vector.tensor_scalar(out=w[:, j, :], in0=src, scalar1=w_scale[:, g, j : j + 1], scalar2=None, op0=ALU.mult)
+                    else:
+                        nc.scalar.activation(out=w[:, j, :], in_=src, func=ACT.Copy, scale=w_scale[:, g, j : j + 1])
+                wide[key] = w
+            elif op == "I":
+                c0, width = BLOCKS[key[2]]
+                t = ring.tile([P, 2048], BF16, name="grouped", tag="grouped", bufs=8, align_bytes=64)
+                if key[0] in "UR":
+                    src = (raw[key] if key[0] == "U" else wide[key])[:].rearrange("p j (m t) -> p m j t", t=4)
+                    dst = t[:].rearrange("p (t m j) -> p m j t", t=4, j=4)
+                else:
+                    src = raw[key[0:2]][:, :, c0 : c0 + width].rearrange("p j (c i) -> p c j i", i=4)
+                    dst = t[:, 0 : 4 * width].rearrange("p (c i j) -> p c j i", i=4, j=4)
+                if engine == "v":
+                    nc.vector.tensor_copy(out=dst, in_=src)
+                else:
+                    nc.scalar.copy(out=dst, in_=src)
+                grouped[key] = t
+            elif op == "Q":
+                if key[0] in "hx":
+                    g = int(key[1])
+                    quant(key, turned[key[0]][:, g * 2048 : (g + 1) * 2048], 512)
+                elif key[0] == "g":
+                    quant(key, gated[key[1]][:], 512)
+                else:
+                    width = BLOCKS[key[2]][1]
+                    quant(key, grouped[key][:, 0 : 4 * width], width)
+            elif op == "m":
+                for t in range(4):
+                    bank = ("lo" if key[2] == "a" else "hi") + str(t)
+                    moving = ("h" if key[0] == "U" else "x") + key[1]
+                    mx("s%s%d" % (key[2], t), bank, B, key, slice(t * P, (t + 1) * P), moving, B, 4)
+            elif op == "s":
+                block, t = key[0], int(key[1])
+                g = "ab".index(block)
+                nc.scalar.activation(out=gate[block][:, t, :], in_=acc["s" + key][:], func=ACT.Sigmoid, bias=br[:, g, t : t + 1])
+            elif op == "g":
+                block, half = key[0], int(key[1])
+                g = "ab".index(block)
+                toks = slice(half * 256, half * 256 + 256)
+                hview = turned["h"][:].rearrange("p (g n t) -> p g n t", g=2, t=4)[:, g, toks, :]
+                gview = gated[block][:].rearrange("p (n t) -> p n t", t=4)[:, toks, :]
+                nc.vector.tensor_tensor(out=gview, in0=hview, in1=gate[block][:, :, toks].rearrange("p t n -> p n t"), op=ALU.mult)
+            elif op == "n":
+                chunk, t = key.split("_")
+                left = ("x" + chunk[1]) if chunk[0] == "H" else ("g" + "ab"[int(chunk[1])])
+                width = BLOCKS[chunk[2]][1]
+                bank = ("hi" if chunk[2] == "1" else "lo") + t
+                mx("b%s%s" % (chunk[2], t), bank, width, left, slice(int(t) * P, (int(t) + 1) * P), chunk, width, 4)
+            elif op == "b":
+                c0, width = BLOCKS[key[0]]
+                r = ring.tile([P, 512], F32, name="res", tag="res", bufs=8)
+                nc.vector.tensor_tensor(out=r[:, 0:width], in0=acc["b" + key][:], in1=bh[:, c0 : c0 + width], op=ALU.add)
+                res[key] = r
+            elif op == "t":
+                c0, width = BLOCKS[key[0]]
+                t = int(key[1])
+                r = res[key]
+                nc.scalar.activation(out=r[:, 0:width], in_=r[:, 0:width], func=ACT.Tanh)
+                nc.sync.dma_start(out=out[t * P : (t + 1) * P, c0 : c0 + width], in_=r[:, 0:width])

@@ -12,199 +12,351 @@ FP8X4 = mybir.dt.float8_e4m3fn_x4
 ACT = mybir.ActivationFunctionType
 ALU = mybir.AluOpType
 
-B, K, H = 512, 1024, 1024
-FLOPS = 4 * 2 * B * K * H
-P = 128
-PASS = 512
+TOKENS, FEATURES, HIDDEN = 512, 1024, 1024
+FLOPS = 2 * TOKENS * HIDDEN * (2 * FEATURES + 2 * HIDDEN)
 
-LOADS = "R0 R1 U1a x3 h2 x1 U1b h3 h1 U0a x0 x2 h0 H0 U0b H1 V0 V1"
-ORDER = (
-    "WR0b/v WR0a/s WR1b/v WR1a/s IR0b/v IR1b/v IU1a/s IR0a/v Th3 QR1b Tx3 Tx1 QR0a IR1a/s Th1 QU1a "
-    "IU1b/v Tx2 Th2 Cx2/s Ch1/v Tx0 Cx1/s Cx3/v Th0 Ch2/s QR1a Ch0/s IU0a/v Cx0/s Ch3/s Qx0 IU0b/s "
-    "Qx1 mR0a Qh1 QR0b mR1a Qh0 IH00/s QU0b mU1a QU0a mU0b IH10/v mU0a IH11/s IV00/v mR1b sa3 QH10 "
-    "sa2 QU1b mR0b sa0 QV00 sa1 QH11 mU1b IH01/s ga0 sb3 IV01/v sb1 ga1 sb0 IV12/s IH12/v QH00 sb2 "
-    "QV01 Qga IV10/s nH11_2 nH00_1 gb1 nH00_0 nV00_1 nV01_3 nH10_0 nH00_2 gb0 nV00_2 nH10_1 nV01_1 "
-    "IV11/s nV00_3 Qgb nV00_0 nH10_3 QV10 nV01_0 nH10_2 IV02/s nH00_3 QH01 nH11_1 nV10_3 QV11 nV10_1 "
-    "QV12 nH01_2 b03 nV11_1 IH02/s nH01_3 nV11_2 nV10_2 QH12 nH11_0 nV10_0 b02 t03 b00 nV12_2 nH12_3 "
-    "nV11_0 t02 nV01_2 QV02 b01 nV02_2 t00 nV12_3 nH01_0 nV02_0 b12 nV02_3 t01 nH11_3 QH02 nH01_1 "
-    "nH12_2 b11 nV12_0 t12 nV12_1 b10 nV11_3 t11 nH02_0 b13 nH02_2 t10 nH12_0 b22 nH12_1 t13 nV02_1 "
-    "b20 nH02_3 t22 nH02_1 b23 t20 b21 t23 t21 "
-)
-BLOCKS = {"a": (0, 512), "b": (512, 512), "0": (0, 512), "1": (512, 256), "2": (768, 256)}
+P = 128
+PACK = 4
+HALF = P * PACK
+TOKEN_TILES = TOKENS // P
+GATE_TILES = 4
+PASSES = 4
+RUN = 4
+
+COLUMNS = {"a": (0, 512), "b": (512, 512), "0": (0, 512), "1": (512, 256), "2": (768, 256)}
+GATE_HALF = {"a": 0, "b": 1}
 
 
 def tile_joint_gru_pa_kernel(tc, joint_h, mgn_h, W_r_bytes, W_r_scale, W_h, U_r, U_h, b_r, b_h, out):
     nc = tc.nc
+    tokens_in = {"joint_h": joint_h, "mgn_h": mgn_h}
+    weights_in = {"U_r": U_r, "W_h": W_h, "U_h": U_h}
+    partner = {"W_r": "mgn_h", "U_r": "joint_h", "W_h": "mgn_h", "U_h": "g"}
+
     with ExitStack() as ctx:
         keep = ctx.enter_context(tc.tile_pool(name="keep", bufs=1))
         ring = ctx.enter_context(tc.tile_pool(name="ring", bufs=8))
         psum = ctx.enter_context(tc.psum_pool(name="psum", bufs=1))
 
-        ident = keep.tile([P, P], F32, name="ident")
-        make_identity(nc, ident[:])
+        ident_f32 = keep.tile([P, P], F32, name="ident_f32")
+        make_identity(nc, ident_f32[:])
+        ident_bf16 = keep.tile([P, P], BF16, name="ident_bf16")
+        make_identity(nc, ident_bf16[:])
         warm = keep.tile([P, 1], F32, name="warm")
         nc.vector.memset(warm[:], 0.0)
 
         ctx.enter_context(tc.manual_schedule())
+
+        byte_scale = keep.tile([P, 2, PACK], F32, name="byte_scale")
+        nc.scalar.dma_start(out=byte_scale[:], in_=W_r_scale.rearrange("(g p j) o -> p g (j o)", g=2, j=PACK))
         nc.scalar.activation(out=warm[:], in_=warm[:], func=ACT.Sigmoid)
-        w_scale = keep.tile([P, 2, 4], F32, name="w_scale")
-        nc.scalar.dma_start(out=w_scale[:], in_=W_r_scale.rearrange("(g p j) o -> p g (j o)", g=2, j=4))
-        br = keep.tile([P, 2, 4], BF16, name="br")
-        nc.scalar.dma_start(out=br[:], in_=b_r.rearrange("(g p t) -> p g t", g=2, t=4))
 
-        raw = {}
-        for key in LOADS.split():
-            kind, g = key[0], int(key[1])
-            rows = slice(g * PASS, (g + 1) * PASS)
-            if kind in "hx":
-                source = joint_h if kind == "h" else mgn_h
-                t = keep.tile([P, K], BF16, name="raw_" + key)
-                nc.sync.dma_start(out=t[:], in_=source[g * P : (g + 1) * P, :])
-                raw[key] = t
-            elif kind == "R":
-                t = keep.tile([P, 4, H], U8, name="raw_" + key)
-                view = W_r_bytes[rows, :].rearrange("(p j) c -> p j c", j=4)
-                if g == 0:
-                    for j in range(4):
-                        nc.sync.dma_start(out=t[:, j, :], in_=view[:, j, :])
-                else:
-                    nc.sync.dma_start(out=t[:], in_=view)
-                raw[key] = t
-            elif kind == "U":
-                c0, width = BLOCKS[key[2]]
-                t = keep.tile([P, 4, width], BF16, name="raw_" + key)
-                nc.sync.dma_start(out=t[:], in_=U_r[rows, c0 : c0 + width].rearrange("(p j) c -> p j c", j=4))
-                raw[key] = t
-            else:
-                source = W_h if kind == "H" else U_h
-                t = keep.tile([P, 4, H], BF16, name="raw_" + key)
-                nc.sync.dma_start(out=t[:], in_=source[rows, :].rearrange("(p j) c -> p j c", j=4))
-                raw[key] = t
-        bh = keep.tile([P, H], BF16, name="bh")
-        nc.sync.dma_start(out=bh[:], in_=b_h.partition_broadcast(P))
-
+        raw_tokens = {}
+        raw_weights = {}
         turned = {}
-        for k in "hx":
-            turned[k] = keep.tile([P, 2 * B * 4], BF16, name="turned_" + k, align_bytes=64)
-        gate = {}
-        for k in "ab":
-            gate[k] = keep.tile([P, 4, B], F32, name="gate_" + k)
-        gated = {}
-        for k in "ab":
-            gated[k] = keep.tile([P, B * 4], BF16, name="gated_" + k, align_bytes=64)
-        wide = {}
+        widened = {}
+        woven = {}
         grouped = {}
         codes = {}
-        turning = {}
-        acc = {}
+        gate = {}
+        gated = {}
+        sums = {}
         passes = {}
-        res = {}
+        result = {}
 
-        def quant(key, src, width):
-            c = keep.tile([P, width], U32, name="codes_" + key, align_bytes=64)
-            s = keep.tile([P, width], U8, name="scales_" + key, align_bytes=64)
-            nc.vector.quantize_mx(out=c[:].bitcast(FP8X4), scales=s[:], in_=src)
-            codes[key] = (c, s)
+        def load_codes(g, pieces):
+            t = keep.tile([P, PACK, HIDDEN], U8, name="bytes_%d" % g)
+            rows = W_r_bytes[g * HALF : (g + 1) * HALF, :].rearrange("(p j) c -> p j c", j=PACK)
+            step = PACK // pieces
+            for j in range(0, PACK, step):
+                nc.sync.dma_start(out=t[:, j : j + step, :], in_=rows[:, j : j + step, :])
+            raw_weights["W_r", g] = t
 
-        def mx(key, bank, width, left, lcols, right, n, total):
-            if key not in passes:
-                passes[key] = 0
-                acc[key] = psum.tile([P, width], F32, name="acc_" + key, tag=bank)
-            done = passes[key]
-            passes[key] = done + 1
-            nc.tensor.matmul_mx(
-                out=acc[key][:],
-                lhsT=codes[left][0][:, lcols].bitcast(FP8X4),
-                lhsT_scale=codes[left][1][:, lcols],
-                rhs=codes[right][0][:, 0:n].bitcast(FP8X4),
-                rhs_scale=codes[right][1][:, 0:n],
-                start=(done == 0),
-                stop=(done == total - 1),
-            )
+        def load_weights(weight, g):
+            t = keep.tile([P, PACK, HIDDEN], BF16, name="raw_%s_%d" % (weight, g))
+            rows = weights_in[weight][g * HALF : (g + 1) * HALF, :]
+            nc.sync.dma_start(out=t[:], in_=rows.rearrange("(p j) c -> p j c", j=PACK))
+            raw_weights[weight, g] = t
 
-        for token in ORDER.split():
-            op = token[0]
-            engine = token[-1] if "/" in token else ""
-            key = token[1:].split("/")[0]
-            if op == "T":
-                t = psum.tile([P, 2, 2, P], F32, name="turning_" + key, tag=("hi" if key[0] == "h" else "lo") + key[1])
-                words = raw[key][:].bitcast(F32)
+        def load_tokens(operand, pair):
+            t = keep.tile([P, 2, FEATURES], BF16, name="raw_%s_%d" % (operand, pair))
+            rows = tokens_in[operand][pair * 2 * P : (pair + 1) * 2 * P, :]
+            nc.sync.dma_start(out=t[:], in_=rows.rearrange("(i p) k -> p i k", i=2))
+            for i in range(2):
+                raw_tokens[operand, 2 * pair + i] = t[:, i, :]
+
+        turning = {}
+
+        def turn(operand, pair):
+            for tile in (2 * pair, 2 * pair + 1):
+                bank = psum.tile([P, 2, 2, P], F32, name="turning_%s_%d" % (operand, tile), tag="lo%d" % (len(turning) % 4))
+                words = raw_tokens[operand, tile].bitcast(F32)
                 for g in range(2):
                     for u in range(2):
-                        nc.tensor.transpose(t[:, g, u, :], words[:, 256 * g + u : 256 * (g + 1) : 2], ident[:])
-                turning[key] = t
-            elif op == "C":
-                i = int(key[1])
-                dst = turned[key[0]][:].bitcast(F32).rearrange("p (g r u) -> p g r u", g=2, u=2)[:, :, i * P : (i + 1) * P, :]
-                src = turning[key][:].rearrange("p g u r -> p g r u")
-                if engine == "v":
-                    nc.vector.tensor_copy(out=dst, in_=src)
-                else:
-                    nc.scalar.copy(out=dst, in_=src)
-            elif op == "W":
-                g = int(key[1])
-                c0, width = BLOCKS[key[2]]
-                w = ring.tile([P, 4, 512], BF16, name="wide", tag="wide", bufs=4)
-                for j in range(4):
-                    src = raw["R" + key[1]][:, j, c0 : c0 + width].bitcast(FP8)
-                    if engine == "v":
-                        nc.vector.tensor_scalar(out=w[:, j, :], in0=src, scalar1=w_scale[:, g, j : j + 1], scalar2=None, op0=ALU.mult)
+                        nc.tensor.transpose(bank[:, g, u, :], words[:, g * 256 + u : (g + 1) * 256 : 2], ident_f32[:])
+                turning[operand, tile] = bank
+
+        def take_turned(copy, operand, pair):
+            if operand not in turned:
+                turned[operand] = keep.tile([P, 2 * TOKENS * PACK], BF16, name="turned_" + operand, align_bytes=64)
+            words = turned[operand][:].bitcast(F32).rearrange("p (g n u) -> p g n u", g=2, u=2)
+            for tile in (2 * pair, 2 * pair + 1):
+                copy(
+                    out=words[:, :, tile * P : (tile + 1) * P, :],
+                    in_=turning[operand, tile][:].rearrange("p g u n -> p g n u"),
+                )
+
+        def widen(chunk, one_row):
+            weight, g, block = chunk
+            first, width = COLUMNS[block]
+            t = ring.tile([P, PACK, width], BF16, name="widened", tag="widened", bufs=4)
+            for j in range(PACK):
+                one_row(t[:, j, :], raw_weights[weight, g][:, j, first : first + width].bitcast(FP8), byte_scale[:, g, j : j + 1])
+            widened[chunk] = t
+
+        def widen_on_vector(chunk):
+            widen(chunk, lambda o, i, s: nc.vector.tensor_scalar(out=o, in0=i, scalar1=s, scalar2=None, op0=ALU.mult))
+
+        def widen_on_scalar(chunk):
+            widen(chunk, lambda o, i, s: nc.scalar.activation(out=o, in_=i, func=ACT.Copy, scale=s))
+
+        def bf16_rows(chunk):
+            weight, g, block = chunk
+            first, width = COLUMNS[block]
+            if weight == "W_r":
+                return widened[chunk][:]
+            return raw_weights[weight, g][:, :, first : first + width]
+
+        def new_grouped(chunk):
+            grouped[chunk] = ring.tile([P, HALF * PACK], BF16, name="grouped", tag="grouped", align_bytes=64)
+            return grouped[chunk][:, 0 : COLUMNS[chunk[2]][1] * PACK]
+
+        def interleave(copy, chunk):
+            rows = bf16_rows(chunk)
+            places = new_grouped(chunk)
+            if chunk[2] in GATE_HALF:
+                copy(
+                    out=places.rearrange("p (t m j) -> p m j t", t=GATE_TILES, j=PACK),
+                    in_=rows.rearrange("p j (m t) -> p m j t", t=GATE_TILES),
+                )
+            else:
+                copy(
+                    out=places.rearrange("p (c i j) -> p c j i", i=RUN, j=PACK),
+                    in_=rows.rearrange("p j (c i) -> p c j i", i=RUN),
+                )
+
+        def weave(chunk):
+            rows = bf16_rows(chunk)
+            first_bank = len(woven) % 2 * 2
+            woven[chunk] = []
+            for part in range(2):
+                bank = psum.tile([P, 256 * PACK], BF16, name="woven_%d" % part, tag="hi%d" % (first_bank + part))
+                for u in range(2):
+                    two_rows = rows[:, 2 * u : 2 * u + 2, part * 256 : (part + 1) * 256]
+                    if chunk[2] in GATE_HALF:
+                        moving = two_rows.rearrange("p j (m t) -> p m t j", t=GATE_TILES)
+                        places = bank[:].rearrange("p (t m j) -> p m t j", t=GATE_TILES, j=PACK)[:, :, :, 2 * u : 2 * u + 2]
                     else:
-                        nc.scalar.activation(out=w[:, j, :], in_=src, func=ACT.Copy, scale=w_scale[:, g, j : j + 1])
-                wide[key] = w
-            elif op == "I":
-                c0, width = BLOCKS[key[2]]
-                t = ring.tile([P, 2048], BF16, name="grouped", tag="grouped", bufs=8, align_bytes=64)
-                if key[0] in "UR":
-                    src = (raw[key] if key[0] == "U" else wide[key])[:].rearrange("p j (m t) -> p m j t", t=4)
-                    dst = t[:].rearrange("p (t m j) -> p m j t", t=4, j=4)
+                        moving = two_rows.rearrange("p j c -> p c j")
+                        places = bank[:].rearrange("p (c j) -> p c j", j=PACK)[:, :, 2 * u : 2 * u + 2]
+                    nc.tensor.matmul(places, lhsT=ident_bf16[:], rhs=moving, start=True, stop=True)
+                woven[chunk].append(bank)
+
+        def take_woven(copy, chunk):
+            places = new_grouped(chunk)
+            for part in range(2):
+                bank = woven[chunk][part][:]
+                if chunk[2] in GATE_HALF:
+                    columns = places.rearrange("p (t m j) -> p t m j", t=GATE_TILES, j=PACK)[:, :, part * 64 : (part + 1) * 64, :]
+                    copy(out=columns, in_=bank.rearrange("p (t m j) -> p t m j", t=GATE_TILES, j=PACK))
                 else:
-                    src = raw[key[0:2]][:, :, c0 : c0 + width].rearrange("p j (c i) -> p c j i", i=4)
-                    dst = t[:, 0 : 4 * width].rearrange("p (c i j) -> p c j i", i=4, j=4)
-                if engine == "v":
-                    nc.vector.tensor_copy(out=dst, in_=src)
-                else:
-                    nc.scalar.copy(out=dst, in_=src)
-                grouped[key] = t
-            elif op == "Q":
-                if key[0] in "hx":
-                    g = int(key[1])
-                    quant(key, turned[key[0]][:, g * 2048 : (g + 1) * 2048], 512)
-                elif key[0] == "g":
-                    quant(key, gated[key[1]][:], 512)
-                else:
-                    width = BLOCKS[key[2]][1]
-                    quant(key, grouped[key][:, 0 : 4 * width], width)
-            elif op == "m":
-                for t in range(4):
-                    bank = ("lo" if key[2] == "a" else "hi") + str(t)
-                    moving = ("h" if key[0] == "U" else "x") + key[1]
-                    mx("s%s%d" % (key[2], t), bank, B, key, slice(t * P, (t + 1) * P), moving, B, 4)
-            elif op == "s":
-                block, t = key[0], int(key[1])
-                g = "ab".index(block)
-                nc.scalar.activation(out=gate[block][:, t, :], in_=acc["s" + key][:], func=ACT.Sigmoid, bias=br[:, g, t : t + 1])
-            elif op == "g":
-                block, half = key[0], int(key[1])
-                g = "ab".index(block)
-                toks = slice(half * 256, half * 256 + 256)
-                hview = turned["h"][:].rearrange("p (g n t) -> p g n t", g=2, t=4)[:, g, toks, :]
-                gview = gated[block][:].rearrange("p (n t) -> p n t", t=4)[:, toks, :]
-                nc.vector.tensor_tensor(out=gview, in0=hview, in1=gate[block][:, :, toks].rearrange("p t n -> p n t"), op=ALU.mult)
-            elif op == "n":
-                chunk, t = key.split("_")
-                left = ("x" + chunk[1]) if chunk[0] == "H" else ("g" + "ab"[int(chunk[1])])
-                width = BLOCKS[chunk[2]][1]
-                bank = ("hi" if chunk[2] == "1" else "lo") + t
-                mx("b%s%s" % (chunk[2], t), bank, width, left, slice(int(t) * P, (int(t) + 1) * P), chunk, width, 4)
-            elif op == "b":
-                c0, width = BLOCKS[key[0]]
-                r = ring.tile([P, 512], F32, name="res", tag="res", bufs=8)
-                nc.vector.tensor_tensor(out=r[:, 0:width], in0=acc["b" + key][:], in1=bh[:, c0 : c0 + width], op=ALU.add)
-                res[key] = r
-            elif op == "t":
-                c0, width = BLOCKS[key[0]]
-                t = int(key[1])
-                r = res[key]
-                nc.scalar.activation(out=r[:, 0:width], in_=r[:, 0:width], func=ACT.Tanh)
-                nc.sync.dma_start(out=out[t * P : (t + 1) * P, c0 : c0 + width], in_=r[:, 0:width])
+                    copy(out=places[:, part * 256 * PACK : (part + 1) * 256 * PACK], in_=bank)
+
+        def quantize(key, name, source, width):
+            c = keep.tile([P, width], U32, name="codes_" + name, align_bytes=64)
+            s = keep.tile([P, width], U8, name="scales_" + name, align_bytes=64)
+            nc.vector.quantize_mx(out=c[:].bitcast(FP8X4), scales=s[:], in_=source)
+            codes[key] = (c, s)
+
+        def quantize_turned(operand, g):
+            size = TOKENS * PACK
+            quantize((operand, g), "%s_%d" % (operand, g), turned[operand][:, g * size : (g + 1) * size], TOKENS)
+
+        def quantize_gated(block):
+            g = GATE_HALF[block]
+            quantize(("g", g), "g_%d" % g, gated[block][:], TOKENS)
+
+        def quantize_weights(chunk):
+            width = COLUMNS[chunk[2]][1]
+            quantize(chunk, "%s_%d_%s" % chunk, grouped[chunk][:, 0 : width * PACK], width)
+
+        def one_pass(key, bank, stationary, columns, moving):
+            width = codes[moving][0].shape[1]
+            if key not in sums:
+                sums[key] = psum.tile([P, width], F32, name="sum_%s_%d" % key, tag=bank)
+                passes[key] = 0
+            passes[key] += 1
+            nc.tensor.matmul_mx(
+                out=sums[key][:],
+                lhsT=codes[stationary][0][:, columns].bitcast(FP8X4),
+                lhsT_scale=codes[stationary][1][:, columns],
+                rhs=codes[moving][0][:].bitcast(FP8X4),
+                rhs_scale=codes[moving][1][:],
+                start=(passes[key] == 1),
+                stop=(passes[key] == PASSES),
+            )
+
+        def gate_matmuls(chunk):
+            weight, g, block = chunk
+            for t in range(GATE_TILES):
+                one_pass((block, t), "lo%d" % t, chunk, slice(t * P, (t + 1) * P), (partner[weight], g))
+
+        def gate_sigmoid(block):
+            gate[block] = keep.tile([P, GATE_TILES, TOKENS], F32, name="gate_" + block)
+            for t in range(GATE_TILES):
+                bias = gate_bias[:, GATE_HALF[block], t : t + 1]
+                nc.scalar.activation(out=gate[block][:, t, :], in_=sums[block, t][:], func=ACT.Sigmoid, bias=bias)
+
+        def gate_product(block):
+            g = GATE_HALF[block]
+            gated[block] = keep.tile([P, TOKENS * PACK], BF16, name="gated_" + block, align_bytes=64)
+            tokens = TOKENS // 2
+            for part in range(2):
+                first = part * tokens * PACK
+                state = turned["joint_h"][:, g * TOKENS * PACK + first : g * TOKENS * PACK + first + tokens * PACK]
+                nc.vector.tensor_tensor(
+                    out=gated[block][:, first : first + tokens * PACK].rearrange("p (n i t) -> p n t i", i=RUN, t=GATE_TILES),
+                    in0=state.rearrange("p (n i t) -> p n t i", i=RUN, t=GATE_TILES),
+                    in1=gate[block][:, :, part * tokens : (part + 1) * tokens].rearrange("p t (n i) -> p n t i", i=RUN),
+                    op=ALU.mult,
+                )
+
+        def out_matmuls(chunk):
+            weight, g, block = chunk
+            banks = "lo" if block == "1" else "hi"
+            for tile in range(TOKEN_TILES):
+                one_pass((block, tile), "%s%d" % (banks, tile), (partner[weight], g), slice(tile * P, (tile + 1) * P), chunk)
+
+        def add_bias(block):
+            first, width = COLUMNS[block]
+            for tile in range(TOKEN_TILES):
+                result[block, tile] = ring.tile([P, 512], F32, name="result", tag="result")
+                nc.vector.tensor_tensor(
+                    out=result[block, tile][:, 0:width], in0=sums[block, tile][:], in1=out_bias[:, first : first + width], op=ALU.add
+                )
+
+        def tanh_and_store(block):
+            first, width = COLUMNS[block]
+            for tile in range(TOKEN_TILES):
+                t = result[block, tile][:, 0:width]
+                nc.scalar.activation(out=t, in_=t, func=ACT.Tanh)
+                nc.sync.dma_start(out=out[tile * P : (tile + 1) * P, first : first + width], in_=t)
+
+        load_codes(1, 4)
+        load_codes(0, 1)
+        load_tokens("mgn_h", 1)
+        load_tokens("joint_h", 0)
+        load_tokens("joint_h", 1)
+        load_tokens("mgn_h", 0)
+        load_weights("U_r", 0)
+        load_weights("U_r", 1)
+        gate_bias = keep.tile([P, 2, GATE_TILES], BF16, name="gate_bias")
+        nc.sync.dma_start(out=gate_bias[:], in_=b_r.rearrange("(g p t) -> p g t", g=2, t=GATE_TILES))
+        load_weights("U_h", 0)
+        load_weights("U_h", 1)
+        load_weights("W_h", 0)
+        load_weights("W_h", 1)
+        out_bias = keep.tile([P, HIDDEN], BF16, name="out_bias")
+        nc.sync.dma_start(out=out_bias[:], in_=b_h.partition_broadcast(P))
+
+        widen_on_vector(("W_r", 1, "b"))
+        widen_on_scalar(("W_r", 1, "a"))
+        widen_on_vector(("W_r", 0, "a"))
+        weave(("W_r", 1, "b"))
+        widen_on_scalar(("W_r", 0, "b"))
+        interleave(nc.vector.tensor_copy, ("W_r", 1, "a"))
+        interleave(nc.vector.tensor_copy, ("W_r", 0, "a"))
+        turn("joint_h", 0)
+        take_woven(nc.scalar.copy, ("W_r", 1, "b"))
+        interleave(nc.vector.tensor_copy, ("W_r", 0, "b"))
+        turn("joint_h", 1)
+        take_turned(nc.scalar.copy, "joint_h", 0)
+        turn("mgn_h", 1)
+        quantize_weights(("W_r", 0, "a"))
+        take_turned(nc.scalar.copy, "joint_h", 1)
+        quantize_weights(("W_r", 0, "b"))
+        quantize_weights(("W_r", 1, "b"))
+        take_turned(nc.scalar.copy, "mgn_h", 1)
+        turn("mgn_h", 0)
+        quantize_turned("joint_h", 0)
+        quantize_turned("joint_h", 1)
+        interleave(nc.scalar.copy, ("U_r", 0, "a"))
+        take_turned(nc.vector.tensor_copy, "mgn_h", 0)
+        weave(("U_r", 0, "b"))
+        quantize_weights(("W_r", 1, "a"))
+        quantize_turned("mgn_h", 0)
+        interleave(nc.scalar.copy, ("U_r", 1, "b"))
+        interleave(nc.vector.tensor_copy, ("U_r", 1, "a"))
+        gate_matmuls(("W_r", 0, "a"))
+        quantize_weights(("U_r", 0, "a"))
+        quantize_turned("mgn_h", 1)
+        gate_matmuls(("U_r", 0, "a"))
+        take_woven(nc.scalar.copy, ("U_r", 0, "b"))
+        quantize_weights(("U_r", 1, "a"))
+        quantize_weights(("U_r", 1, "b"))
+        gate_matmuls(("W_r", 1, "a"))
+        interleave(nc.scalar.copy, ("U_h", 0, "0"))
+        quantize_weights(("U_r", 0, "b"))
+        gate_matmuls(("U_r", 1, "a"))
+        interleave(nc.vector.tensor_copy, ("U_h", 0, "1"))
+        interleave(nc.vector.tensor_copy, ("U_h", 1, "1"))
+        weave(("U_h", 1, "0"))
+        quantize_weights(("U_h", 0, "1"))
+        gate_sigmoid("a")
+        quantize_weights(("U_h", 1, "1"))
+        quantize_weights(("U_h", 0, "0"))
+        interleave(nc.vector.tensor_copy, ("U_h", 0, "2"))
+        interleave(nc.vector.tensor_copy, ("W_h", 0, "1"))
+        interleave(nc.scalar.copy, ("W_h", 0, "0"))
+        quantize_weights(("U_h", 0, "2"))
+        gate_matmuls(("U_r", 0, "b"))
+        quantize_weights(("W_h", 0, "1"))
+        gate_product("a")
+        gate_matmuls(("W_r", 1, "b"))
+        gate_matmuls(("W_r", 0, "b"))
+        interleave(nc.scalar.copy, ("W_h", 1, "1"))
+        interleave(nc.vector.tensor_copy, ("W_h", 1, "0"))
+        gate_matmuls(("U_r", 1, "b"))
+        take_woven(nc.scalar.copy, ("U_h", 1, "0"))
+        quantize_weights(("W_h", 0, "0"))
+        gate_sigmoid("b")
+        quantize_gated("a")
+        out_matmuls(("W_h", 0, "0"))
+        quantize_weights(("W_h", 1, "0"))
+        quantize_weights(("U_h", 1, "0"))
+        out_matmuls(("U_h", 0, "0"))
+        quantize_weights(("W_h", 1, "1"))
+        interleave(nc.scalar.copy, ("U_h", 1, "2"))
+        gate_product("b")
+        out_matmuls(("W_h", 1, "0"))
+        interleave(nc.scalar.copy, ("W_h", 1, "2"))
+        out_matmuls(("W_h", 0, "1"))
+        out_matmuls(("W_h", 1, "1"))
+        quantize_weights(("U_h", 1, "2"))
+        interleave(nc.scalar.copy, ("W_h", 0, "2"))
+        out_matmuls(("U_h", 0, "1"))
+        quantize_gated("b")
+        quantize_weights(("W_h", 1, "2"))
+        out_matmuls(("U_h", 1, "0"))
+        add_bias("0")
+        out_matmuls(("U_h", 1, "1"))
+        tanh_and_store("0")
+        out_matmuls(("U_h", 0, "2"))
+        quantize_weights(("W_h", 0, "2"))
+        add_bias("1")
+        out_matmuls(("W_h", 1, "2"))
+        tanh_and_store("1")
+        out_matmuls(("U_h", 1, "2"))
+        out_matmuls(("W_h", 0, "2"))
+        add_bias("2")
+        tanh_and_store("2")

from contextlib import ExitStack

import concourse.mybir as mybir
from concourse.masks import make_identity

F32 = mybir.dt.float32
BF16 = mybir.dt.bfloat16
U32 = mybir.dt.uint32
U8 = mybir.dt.uint8
FP8 = mybir.dt.float8_e4m3fn
FP8X4 = mybir.dt.float8_e4m3fn_x4
ACT = mybir.ActivationFunctionType
ALU = mybir.AluOpType

TOKENS, FEATURES, HIDDEN = 512, 1024, 1024
FLOPS = 2 * TOKENS * HIDDEN * (2 * FEATURES + 2 * HIDDEN)

P = 128
PACK = 4
HALF = P * PACK
TOKEN_TILES = TOKENS // P
GATE_TILES = 4
PASSES = 4
RUN = 4

COLUMNS = {"a": (0, 512), "b": (512, 512), "0": (0, 512), "1": (512, 256), "2": (768, 256)}
GATE_HALF = {"a": 0, "b": 1}


def tile_joint_gru_pa_kernel(tc, joint_h, mgn_h, W_r_bytes, W_r_scale, W_h, U_r, U_h, b_r, b_h, out):
    nc = tc.nc
    tokens_in = {"joint_h": joint_h, "mgn_h": mgn_h}
    weights_in = {"U_r": U_r, "W_h": W_h, "U_h": U_h}
    partner = {"W_r": "mgn_h", "U_r": "joint_h", "W_h": "mgn_h", "U_h": "g"}

    with ExitStack() as ctx:
        keep = ctx.enter_context(tc.tile_pool(name="keep", bufs=1))
        ring = ctx.enter_context(tc.tile_pool(name="ring", bufs=8))
        psum = ctx.enter_context(tc.psum_pool(name="psum", bufs=1))

        ident_f32 = keep.tile([P, P], F32, name="ident_f32")
        make_identity(nc, ident_f32[:])
        ident_bf16 = keep.tile([P, P], BF16, name="ident_bf16")
        make_identity(nc, ident_bf16[:])
        warm = keep.tile([P, 1], F32, name="warm")
        nc.vector.memset(warm[:], 0.0)

        ctx.enter_context(tc.manual_schedule())

        byte_scale = keep.tile([P, 2, PACK], F32, name="byte_scale")
        nc.scalar.dma_start(out=byte_scale[:], in_=W_r_scale.rearrange("(g p j) o -> p g (j o)", g=2, j=PACK))
        nc.scalar.activation(out=warm[:], in_=warm[:], func=ACT.Sigmoid)

        raw_tokens = {}
        raw_weights = {}
        turned = {}
        widened = {}
        woven = {}
        grouped = {}
        codes = {}
        gate = {}
        gated = {}
        sums = {}
        passes = {}
        result = {}

        def load_codes(g, pieces):
            t = keep.tile([P, PACK, HIDDEN], U8, name="bytes_%d" % g)
            rows = W_r_bytes[g * HALF : (g + 1) * HALF, :].rearrange("(p j) c -> p j c", j=PACK)
            step = PACK // pieces
            for j in range(0, PACK, step):
                nc.sync.dma_start(out=t[:, j : j + step, :], in_=rows[:, j : j + step, :])
            raw_weights["W_r", g] = t

        def load_weights(weight, g):
            t = keep.tile([P, PACK, HIDDEN], BF16, name="raw_%s_%d" % (weight, g))
            rows = weights_in[weight][g * HALF : (g + 1) * HALF, :]
            nc.sync.dma_start(out=t[:], in_=rows.rearrange("(p j) c -> p j c", j=PACK))
            raw_weights[weight, g] = t

        def load_tokens(operand, pair):
            t = keep.tile([P, 2, FEATURES], BF16, name="raw_%s_%d" % (operand, pair))
            rows = tokens_in[operand][pair * 2 * P : (pair + 1) * 2 * P, :]
            nc.sync.dma_start(out=t[:], in_=rows.rearrange("(i p) k -> p i k", i=2))
            for i in range(2):
                raw_tokens[operand, 2 * pair + i] = t[:, i, :]

        turning = {}

        def turn(operand, pair):
            for tile in (2 * pair, 2 * pair + 1):
                bank = psum.tile([P, 2, 2, P], F32, name="turning_%s_%d" % (operand, tile), tag="lo%d" % (len(turning) % 4))
                words = raw_tokens[operand, tile].bitcast(F32)
                for g in range(2):
                    for u in range(2):
                        nc.tensor.transpose(bank[:, g, u, :], words[:, g * 256 + u : (g + 1) * 256 : 2], ident_f32[:])
                turning[operand, tile] = bank

        def take_turned(copy, operand, pair):
            if operand not in turned:
                turned[operand] = keep.tile([P, 2 * TOKENS * PACK], BF16, name="turned_" + operand, align_bytes=64)
            words = turned[operand][:].bitcast(F32).rearrange("p (g n u) -> p g n u", g=2, u=2)
            for tile in (2 * pair, 2 * pair + 1):
                copy(
                    out=words[:, :, tile * P : (tile + 1) * P, :],
                    in_=turning[operand, tile][:].rearrange("p g u n -> p g n u"),
                )

        def widen(chunk, one_row):
            weight, g, block = chunk
            first, width = COLUMNS[block]
            t = ring.tile([P, PACK, width], BF16, name="widened", tag="widened", bufs=4)
            for j in range(PACK):
                one_row(t[:, j, :], raw_weights[weight, g][:, j, first : first + width].bitcast(FP8), byte_scale[:, g, j : j + 1])
            widened[chunk] = t

        def widen_on_vector(chunk):
            widen(chunk, lambda o, i, s: nc.vector.tensor_scalar(out=o, in0=i, scalar1=s, scalar2=None, op0=ALU.mult))

        def widen_on_scalar(chunk):
            widen(chunk, lambda o, i, s: nc.scalar.activation(out=o, in_=i, func=ACT.Copy, scale=s))

        def bf16_rows(chunk):
            weight, g, block = chunk
            first, width = COLUMNS[block]
            if weight == "W_r":
                return widened[chunk][:]
            return raw_weights[weight, g][:, :, first : first + width]

        def new_grouped(chunk):
            grouped[chunk] = ring.tile([P, HALF * PACK], BF16, name="grouped", tag="grouped", align_bytes=64)
            return grouped[chunk][:, 0 : COLUMNS[chunk[2]][1] * PACK]

        def interleave(copy, chunk):
            rows = bf16_rows(chunk)
            places = new_grouped(chunk)
            if chunk[2] in GATE_HALF:
                copy(
                    out=places.rearrange("p (t m j) -> p m j t", t=GATE_TILES, j=PACK),
                    in_=rows.rearrange("p j (m t) -> p m j t", t=GATE_TILES),
                )
            else:
                copy(
                    out=places.rearrange("p (c i j) -> p c j i", i=RUN, j=PACK),
                    in_=rows.rearrange("p j (c i) -> p c j i", i=RUN),
                )

        def weave(chunk):
            rows = bf16_rows(chunk)
            first_bank = len(woven) % 2 * 2
            woven[chunk] = []
            for part in range(2):
                bank = psum.tile([P, 256 * PACK], BF16, name="woven_%d" % part, tag="hi%d" % (first_bank + part))
                for u in range(2):
                    two_rows = rows[:, 2 * u : 2 * u + 2, part * 256 : (part + 1) * 256]
                    if chunk[2] in GATE_HALF:
                        moving = two_rows.rearrange("p j (m t) -> p m t j", t=GATE_TILES)
                        places = bank[:].rearrange("p (t m j) -> p m t j", t=GATE_TILES, j=PACK)[:, :, :, 2 * u : 2 * u + 2]
                    else:
                        moving = two_rows.rearrange("p j c -> p c j")
                        places = bank[:].rearrange("p (c j) -> p c j", j=PACK)[:, :, 2 * u : 2 * u + 2]
                    nc.tensor.matmul(places, lhsT=ident_bf16[:], rhs=moving, start=True, stop=True)
                woven[chunk].append(bank)

        def take_woven(copy, chunk):
            places = new_grouped(chunk)
            for part in range(2):
                bank = woven[chunk][part][:]
                if chunk[2] in GATE_HALF:
                    columns = places.rearrange("p (t m j) -> p t m j", t=GATE_TILES, j=PACK)[:, :, part * 64 : (part + 1) * 64, :]
                    copy(out=columns, in_=bank.rearrange("p (t m j) -> p t m j", t=GATE_TILES, j=PACK))
                else:
                    copy(out=places[:, part * 256 * PACK : (part + 1) * 256 * PACK], in_=bank)

        def quantize(key, name, source, width):
            c = keep.tile([P, width], U32, name="codes_" + name, align_bytes=64)
            s = keep.tile([P, width], U8, name="scales_" + name, align_bytes=64)
            nc.vector.quantize_mx(out=c[:].bitcast(FP8X4), scales=s[:], in_=source)
            codes[key] = (c, s)

        def quantize_turned(operand, g):
            size = TOKENS * PACK
            quantize((operand, g), "%s_%d" % (operand, g), turned[operand][:, g * size : (g + 1) * size], TOKENS)

        def quantize_gated(block):
            g = GATE_HALF[block]
            quantize(("g", g), "g_%d" % g, gated[block][:], TOKENS)

        def quantize_weights(chunk):
            width = COLUMNS[chunk[2]][1]
            quantize(chunk, "%s_%d_%s" % chunk, grouped[chunk][:, 0 : width * PACK], width)

        def one_pass(key, bank, stationary, columns, moving):
            width = codes[moving][0].shape[1]
            if key not in sums:
                sums[key] = psum.tile([P, width], F32, name="sum_%s_%d" % key, tag=bank)
                passes[key] = 0
            passes[key] += 1
            nc.tensor.matmul_mx(
                out=sums[key][:],
                lhsT=codes[stationary][0][:, columns].bitcast(FP8X4),
                lhsT_scale=codes[stationary][1][:, columns],
                rhs=codes[moving][0][:].bitcast(FP8X4),
                rhs_scale=codes[moving][1][:],
                start=(passes[key] == 1),
                stop=(passes[key] == PASSES),
            )

        def gate_matmuls(chunk):
            weight, g, block = chunk
            for t in range(GATE_TILES):
                one_pass((block, t), "lo%d" % t, chunk, slice(t * P, (t + 1) * P), (partner[weight], g))

        def gate_sigmoid(block):
            gate[block] = keep.tile([P, GATE_TILES, TOKENS], F32, name="gate_" + block)
            for t in range(GATE_TILES):
                bias = gate_bias[:, GATE_HALF[block], t : t + 1]
                nc.scalar.activation(out=gate[block][:, t, :], in_=sums[block, t][:], func=ACT.Sigmoid, bias=bias)

        def gate_product(block):
            g = GATE_HALF[block]
            gated[block] = keep.tile([P, TOKENS * PACK], BF16, name="gated_" + block, align_bytes=64)
            tokens = TOKENS // 2
            for part in range(2):
                first = part * tokens * PACK
                state = turned["joint_h"][:, g * TOKENS * PACK + first : g * TOKENS * PACK + first + tokens * PACK]
                nc.vector.tensor_tensor(
                    out=gated[block][:, first : first + tokens * PACK].rearrange("p (n i t) -> p n t i", i=RUN, t=GATE_TILES),
                    in0=state.rearrange("p (n i t) -> p n t i", i=RUN, t=GATE_TILES),
                    in1=gate[block][:, :, part * tokens : (part + 1) * tokens].rearrange("p t (n i) -> p n t i", i=RUN),
                    op=ALU.mult,
                )

        def out_matmuls(chunk):
            weight, g, block = chunk
            banks = "lo" if block == "1" else "hi"
            for tile in range(TOKEN_TILES):
                one_pass((block, tile), "%s%d" % (banks, tile), (partner[weight], g), slice(tile * P, (tile + 1) * P), chunk)

        def add_bias(block):
            first, width = COLUMNS[block]
            for tile in range(TOKEN_TILES):
                result[block, tile] = ring.tile([P, 512], F32, name="result", tag="result")
                nc.vector.tensor_tensor(
                    out=result[block, tile][:, 0:width], in0=sums[block, tile][:], in1=out_bias[:, first : first + width], op=ALU.add
                )

        def tanh_and_store(block):
            first, width = COLUMNS[block]
            for tile in range(TOKEN_TILES):
                t = result[block, tile][:, 0:width]
                nc.scalar.activation(out=t, in_=t, func=ACT.Tanh)
                nc.sync.dma_start(out=out[tile * P : (tile + 1) * P, first : first + width], in_=t)

        load_codes(1, 4)
        load_codes(0, 1)
        load_tokens("mgn_h", 1)
        load_tokens("joint_h", 0)
        load_tokens("joint_h", 1)
        load_tokens("mgn_h", 0)
        load_weights("U_r", 0)
        load_weights("U_r", 1)
        gate_bias = keep.tile([P, 2, GATE_TILES], BF16, name="gate_bias")
        nc.sync.dma_start(out=gate_bias[:], in_=b_r.rearrange("(g p t) -> p g t", g=2, t=GATE_TILES))
        load_weights("U_h", 0)
        load_weights("U_h", 1)
        load_weights("W_h", 0)
        load_weights("W_h", 1)
        out_bias = keep.tile([P, HIDDEN], BF16, name="out_bias")
        nc.sync.dma_start(out=out_bias[:], in_=b_h.partition_broadcast(P))

        widen_on_vector(("W_r", 1, "b"))
        widen_on_scalar(("W_r", 1, "a"))
        widen_on_vector(("W_r", 0, "a"))
        weave(("W_r", 1, "b"))
        widen_on_scalar(("W_r", 0, "b"))
        interleave(nc.vector.tensor_copy, ("W_r", 1, "a"))
        interleave(nc.vector.tensor_copy, ("W_r", 0, "a"))
        turn("joint_h", 0)
        take_woven(nc.scalar.copy, ("W_r", 1, "b"))
        interleave(nc.vector.tensor_copy, ("W_r", 0, "b"))
        turn("joint_h", 1)
        take_turned(nc.scalar.copy, "joint_h", 0)
        turn("mgn_h", 1)
        quantize_weights(("W_r", 0, "a"))
        take_turned(nc.scalar.copy, "joint_h", 1)
        quantize_weights(("W_r", 0, "b"))
        quantize_weights(("W_r", 1, "b"))
        take_turned(nc.scalar.copy, "mgn_h", 1)
        turn("mgn_h", 0)
        quantize_turned("joint_h", 0)
        quantize_turned("joint_h", 1)
        interleave(nc.scalar.copy, ("U_r", 0, "a"))
        take_turned(nc.vector.tensor_copy, "mgn_h", 0)
        weave(("U_r", 0, "b"))
        quantize_weights(("W_r", 1, "a"))
        quantize_turned("mgn_h", 0)
        interleave(nc.scalar.copy, ("U_r", 1, "b"))
        interleave(nc.vector.tensor_copy, ("U_r", 1, "a"))
        gate_matmuls(("W_r", 0, "a"))
        quantize_weights(("U_r", 0, "a"))
        quantize_turned("mgn_h", 1)
        gate_matmuls(("U_r", 0, "a"))
        take_woven(nc.scalar.copy, ("U_r", 0, "b"))
        quantize_weights(("U_r", 1, "a"))
        quantize_weights(("U_r", 1, "b"))
        gate_matmuls(("W_r", 1, "a"))
        interleave(nc.scalar.copy, ("U_h", 0, "0"))
        quantize_weights(("U_r", 0, "b"))
        gate_matmuls(("U_r", 1, "a"))
        interleave(nc.vector.tensor_copy, ("U_h", 0, "1"))
        interleave(nc.vector.tensor_copy, ("U_h", 1, "1"))
        weave(("U_h", 1, "0"))
        quantize_weights(("U_h", 0, "1"))
        gate_sigmoid("a")
        quantize_weights(("U_h", 1, "1"))
        quantize_weights(("U_h", 0, "0"))
        interleave(nc.vector.tensor_copy, ("U_h", 0, "2"))
        interleave(nc.vector.tensor_copy, ("W_h", 0, "1"))
        interleave(nc.scalar.copy, ("W_h", 0, "0"))
        quantize_weights(("U_h", 0, "2"))
        gate_matmuls(("U_r", 0, "b"))
        quantize_weights(("W_h", 0, "1"))
        gate_product("a")
        gate_matmuls(("W_r", 1, "b"))
        gate_matmuls(("W_r", 0, "b"))
        interleave(nc.scalar.copy, ("W_h", 1, "1"))
        interleave(nc.vector.tensor_copy, ("W_h", 1, "0"))
        gate_matmuls(("U_r", 1, "b"))
        take_woven(nc.scalar.copy, ("U_h", 1, "0"))
        quantize_weights(("W_h", 0, "0"))
        gate_sigmoid("b")
        quantize_gated("a")
        out_matmuls(("W_h", 0, "0"))
        quantize_weights(("W_h", 1, "0"))
        quantize_weights(("U_h", 1, "0"))
        out_matmuls(("U_h", 0, "0"))
        quantize_weights(("W_h", 1, "1"))
        interleave(nc.scalar.copy, ("U_h", 1, "2"))
        gate_product("b")
        out_matmuls(("W_h", 1, "0"))
        interleave(nc.scalar.copy, ("W_h", 1, "2"))
        out_matmuls(("W_h", 0, "1"))
        out_matmuls(("W_h", 1, "1"))
        quantize_weights(("U_h", 1, "2"))
        interleave(nc.scalar.copy, ("W_h", 0, "2"))
        out_matmuls(("U_h", 0, "1"))
        quantize_gated("b")
        quantize_weights(("W_h", 1, "2"))
        out_matmuls(("U_h", 1, "0"))
        add_bias("0")
        out_matmuls(("U_h", 1, "1"))
        tanh_and_store("0")
        out_matmuls(("U_h", 0, "2"))
        quantize_weights(("W_h", 0, "2"))
        add_bias("1")
        out_matmuls(("W_h", 1, "2"))
        tanh_and_store("1")
        out_matmuls(("U_h", 1, "2"))
        out_matmuls(("W_h", 0, "2"))
        add_bias("2")
        tanh_and_store("2")
